import numpy as np
import ml_dtypes


def mxq(x, axis, fmt="e4m3"):
    dtype, down = {"e4m3": (ml_dtypes.float8_e4m3fn, 7), "e5m2": (ml_dtypes.float8_e5m2, 14)}[fmt]
    v = np.moveaxis(np.asarray(x, np.float32).astype(ml_dtypes.bfloat16).astype(np.float64), axis, -1)
    blocks = v.reshape(v.shape[:-1] + (-1, 32))
    amax = np.abs(blocks).max(-1, keepdims=True)
    byte = np.maximum(np.where(amax > 0, np.frexp(amax)[1] - 1 + 127, 0) - down, 1)
    scale = np.exp2(byte - 127.0)
    codes = (blocks / scale).astype(np.float32).astype(dtype).astype(np.float64)
    return np.moveaxis((codes * scale).reshape(v.shape), -1, axis)


WIDE = False


def mx_kscale(k):
    if not WIDE:
        return np.ones(k)
    levels = np.array([10, -10, 5, -5, 0])
    a = np.random.permutation(np.resize(levels, k // 512 * 4)).reshape(k // 512, 4)
    idx = np.arange(k)
    return np.exp2(a[idx // 512, idx % 128 // 32])


BF16 = ml_dtypes.bfloat16


def bf(x):
    return np.asarray(x, np.float32).astype(BF16)


def f64(x):
    return np.asarray(x).astype(np.float64)


E2M1 = np.array([0.0, 0.5, 1.0, 1.5, 2.0, 3.0, 4.0, 6.0, -0.0, -0.5, -1.0, -1.5, -2.0, -3.0, -4.0, -6.0])


def pack_weight(w, fmt):
    k, n = w.shape
    w = f64(bf(w)).reshape(k // 32, 32, n)
    amax = np.abs(w).max(1)
    if fmt == "e4m3":
        byte = np.frexp(amax)[1] - 1 + 127 - 7
    else:
        mant, ex = np.frexp(amax / 6.0)
        byte = np.where(mant > 0.5, ex, ex - 1) + 127
    byte = np.clip(np.where(amax > 0, byte, 1), 1, 254)
    scaled = (w * np.exp2(127.0 - byte)[:, None, :]).reshape(k, n).astype(np.float32)
    by_word = np.ascontiguousarray(scaled.reshape(k // 512, 128, 4, n).transpose(0, 1, 3, 2))
    if fmt == "e4m3":
        words = by_word.astype(ml_dtypes.float8_e4m3fn).view(np.uint8)
    else:
        c = by_word.astype(ml_dtypes.float4_e2m1fn).view(np.uint8) & 0xF
        words = c[..., 0::2] | (c[..., 1::2] << 4)
    return np.ascontiguousarray(words), np.ascontiguousarray(byte.astype(np.uint8).reshape(k // 512, 16, n))


def unpack_weight(words, scales, fmt):
    g, p, n, _ = words.shape
    if fmt == "e4m3":
        vals = np.ascontiguousarray(words).view(ml_dtypes.float8_e4m3fn).astype(np.float64)
    else:
        nib = np.empty((g, p, n, 4), np.uint8)
        nib[..., 0::2] = words & 0xF
        nib[..., 1::2] = words >> 4
        vals = E2M1[nib]
    vals = vals * np.repeat(np.exp2(scales.astype(np.float64) - 127.0), 8, axis=1)[..., None]
    return vals.transpose(0, 1, 3, 2).reshape(g * 512, n)


B, H, NSE = 2048, 512, 1024


def sigmoid(v):
    return 1.0 / (1.0 + np.exp(-v))


def setup_inputs():
    s = mx_kscale(H)
    t = np.exp2(np.round(np.log2(mx_kscale(H)) / 2))
    z_i = bf(np.random.standard_normal((B, H)) * (t * t))
    z_j = bf(np.random.standard_normal((B, H)) * s)
    R = (np.eye(H) + np.random.standard_normal((H, H)) / np.sqrt(H)) / s[None, :]
    R_words, R_scales = pack_weight(np.ascontiguousarray(R.T), "e4m3")
    D = bf((1.0 + 0.3 * np.random.standard_normal((NSE, H))) * 0.9 / H ** 0.25 / t[None, :])
    return {"z_i": z_i,
            "z_j": z_j,
            "R_words": R_words,
            "R_scales": R_scales,
            "D": D}


def reference(z_i, z_j, R_words, R_scales, D):
    Rz_j = mxq(f64(z_j), 1, "e4m3") @ unpack_weight(R_words, R_scales, "e4m3")
    p = f64(z_i) * Rz_j
    d2 = f64(D) * f64(D)
    scores = mxq(p, 1, "e4m3") @ mxq(d2, 1, "e4m3").T
    return sigmoid(scores)

@@ -1,0 +1,195 @@
+from contextlib import ExitStack
+
+import concourse.mybir as mybir
+from concourse.masks import make_identity
+
+BF16 = mybir.dt.bfloat16
+F32 = mybir.dt.float32
+I32 = mybir.dt.int32
+U32 = mybir.dt.uint32
+U8 = mybir.dt.uint8
+FP8X4 = mybir.dt.float8_e4m3fn_x4
+MULT = mybir.AluOpType.mult
+SIGMOID = mybir.ActivationFunctionType.Sigmoid
+SQUARE = mybir.ActivationFunctionType.Square
+
+P = 128
+PACK = 4
+BATCH, HIDDEN, RELATIONS = 2048, 512, 1024
+BANK = 512
+B_TILES = BATCH // P
+R_TILES = RELATIONS // P
+PAIR = 2
+ROUNDS = B_TILES // PAIR
+LOAD_TILES = 4
+WORDS = HIDDEN // 2
+
+FLOPS = 2 * BATCH * HIDDEN * HIDDEN + 2 * BATCH * HIDDEN * RELATIONS
+
+
+def tile_dedicomdecoder_kernel(tc, z_i, z_j, R_words, R_scales, D, out):
+    nc = tc.nc
+    with ExitStack() as ctx:
+        consts = ctx.enter_context(tc.tile_pool(name="consts", bufs=1))
+        inputs = ctx.enter_context(tc.tile_pool(name="inputs", bufs=1))
+        work = ctx.enter_context(tc.tile_pool(name="work", bufs=3))
+        results = ctx.enter_context(tc.tile_pool(name="results", bufs=4))
+        psum_flip = ctx.enter_context(tc.psum_pool(name="psum_flip", bufs=2))
+        psum_rz = ctx.enter_context(tc.psum_pool(name="psum_rz", bufs=2))
+        psum_scores = ctx.enter_context(tc.psum_pool(name="psum_scores", bufs=4))
+
+        zj_rows = z_j.rearrange("(p n) k -> p n k", n=B_TILES)
+        zi_rows = z_i.rearrange("(p n) h -> p n h", n=B_TILES)
+        out_rows = out.rearrange("(p n) r -> p n r", n=B_TILES)
+        d_rows = D.rearrange("(n p) h -> p n h", p=P)
+
+        warm_in = consts.tile([P, 1], F32)
+        warm_out = consts.tile([P, 1], F32)
+        nc.vector.memset(warm_in[:], 0.0)
+        nc.scalar.activation(out=warm_out[:], in_=warm_in[:], func=SIGMOID)
+
+        ident_f32 = consts.tile([P, P], F32)
+        ident_bf16 = consts.tile([P, P], BF16)
+        make_identity(nc, ident_bf16[:])
+        make_identity(nc, ident_f32[:])
+
+        w_words = consts.tile([P, HIDDEN], U32, align_bytes=64)
+        w_scales = consts.tile([P, HIDDEN], U8, align_bytes=64)
+        nc.vector.memset(w_scales[:].bitcast(I32), 0)
+        for r in range(4):
+            nc.sync.dma_start(
+                out=w_scales[:].bitcast(I32)[r:P:32, :], in_=R_scales[0].bitcast(I32)[r:16:4, :]
+            )
+        nc.sync.dma_start(
+            out=w_words[:].bitcast(I32), in_=R_words[0].rearrange("p n t -> p (n t)").bitcast(I32)
+        )
+
+        d_in = [inputs.tile([P, LOAD_TILES, HIDDEN], BF16, name="d_in%d" % c) for c in range(R_TILES // LOAD_TILES)]
+        zj_in = [inputs.tile([P, LOAD_TILES, HIDDEN], BF16, name="zj_in%d" % c) for c in range(B_TILES // LOAD_TILES)]
+        zi_in = [inputs.tile([P, LOAD_TILES, HIDDEN], BF16, name="zi_in%d" % c) for c in range(B_TILES // LOAD_TILES)]
+
+        def load(tiles, rows, c):
+            nc.sync.dma_start(out=tiles[c][:], in_=rows[:, c * LOAD_TILES : (c + 1) * LOAD_TILES, :])
+
+        load(d_in, d_rows, 0)
+        load(zj_in, zj_rows, 0)
+        load(zi_in, zi_rows, 0)
+        load(d_in, d_rows, 1)
+        for c in range(1, B_TILES // LOAD_TILES):
+            load(zj_in, zj_rows, c)
+            load(zi_in, zi_rows, c)
+
+        d2_grouped = consts.tile([P, R_TILES // PAIR, PAIR, P, PACK], BF16, align_bytes=64)
+        d2_words = consts.tile([P, RELATIONS], U32, align_bytes=64)
+        d2_scales = consts.tile([P, RELATIONS], U8, align_bytes=64)
+
+        def prepare_d2(g):
+            d_flip = psum_scores.tile([P, PAIR, PACK, P], BF16, tag="scores")
+            for j in range(PAIR):
+                n = g * PAIR + j
+                for t in range(PACK):
+                    nc.tensor.transpose(
+                        d_flip[:, j, t, :],
+                        d_in[n // LOAD_TILES][:, n % LOAD_TILES, t * P : (t + 1) * P],
+                        ident_bf16[:],
+                    )
+            nc.scalar.activation(
+                out=d2_grouped[:, g], in_=d_flip[:].rearrange("p j t r -> p j r t"), func=SQUARE
+            )
+            cols = slice(g * PAIR * P, (g + 1) * PAIR * P)
+            nc.vector.quantize_mx(
+                out=d2_words[:, cols].bitcast(FP8X4),
+                scales=d2_scales[:, cols],
+                in_=d2_grouped[:, g].rearrange("p j r t -> p (j r t)"),
+            )
+
+        def flip_inputs(i):
+            zj_flip = psum_flip.tile([P, PAIR, 2, P], F32, tag="flip")
+            for j in range(PAIR):
+                n = i * PAIR + j
+                words = zj_in[n // LOAD_TILES][:, n % LOAD_TILES, :].bitcast(F32)
+                for u in range(2):
+                    nc.tensor.transpose(zj_flip[:, j, u, :], words[:, u:WORDS:2], ident_f32[:])
+            zj_grouped = work.tile([P, PAIR * P * PACK], BF16, align_bytes=64)
+            nc.vector.tensor_copy(
+                out=zj_grouped[:].bitcast(F32).rearrange("p (j b u) -> p j b u", j=PAIR, u=2),
+                in_=zj_flip[:].rearrange("p j u b -> p j b u"),
+            )
+            zi_flip = psum_flip.tile([P, PAIR, PACK, P], BF16, tag="flip")
+            for j in range(PAIR):
+                n = i * PAIR + j
+                for t in range(PACK):
+                    nc.tensor.transpose(
+                        zi_flip[:, j, t, :],
+                        zi_in[n // LOAD_TILES][:, n % LOAD_TILES, t * P : (t + 1) * P],
+                        ident_bf16[:],
+                    )
+            zi_t = work.tile([P, PAIR, PACK, P], BF16)
+            nc.vector.tensor_copy(out=zi_t[:], in_=zi_flip[:])
+            zj_words = work.tile([P, PAIR * P], U32, align_bytes=64)
+            zj_scales = work.tile([P, PAIR * P], U8, align_bytes=64)
+            nc.vector.quantize_mx(out=zj_words[:].bitcast(FP8X4), scales=zj_scales[:], in_=zj_grouped[:])
+            return zj_words, zj_scales, zi_t
+
+        def first_product(zj_words, zj_scales, zi_t):
+            p_grouped = work.tile([P, PAIR, P, PACK], BF16, align_bytes=64)
+            for j in range(PAIR):
+                b_cols = slice(j * P, (j + 1) * P)
+                rz = psum_rz.tile([P, PACK, P], F32)
+                for t in range(PACK):
+                    h_cols = slice(t * P, (t + 1) * P)
+                    nc.tensor.matmul_mx(
+                        out=rz[:, t, :],
+                        lhsT=w_words[:, h_cols].bitcast(FP8X4),
+                        lhsT_scale=w_scales[:, h_cols],
+                        rhs=zj_words[:, b_cols].bitcast(FP8X4),
+                        rhs_scale=zj_scales[:, b_cols],
+                        start=True,
+                        stop=True,
+                    )
+                nc.vector.tensor_tensor(
+                    out=p_grouped[:, j],
+                    in0=rz[:].rearrange("p t b -> p b t"),
+                    in1=zi_t[:, j].rearrange("p t b -> p b t"),
+                    op=MULT,
+                )
+            p_words = work.tile([P, PAIR * P], U32, align_bytes=64)
+            p_scales = work.tile([P, PAIR * P], U8, align_bytes=64)
+            nc.vector.quantize_mx(
+                out=p_words[:].bitcast(FP8X4),
+                scales=p_scales[:],
+                in_=p_grouped[:].rearrange("p j b t -> p (j b t)"),
+            )
+            return p_words, p_scales
+
+        def second_product(i, p_words, p_scales):
+            for j in range(PAIR):
+                b_cols = slice(j * P, (j + 1) * P)
+                result = results.tile([P, RELATIONS], F32)
+                for half in range(RELATIONS // BANK):
+                    r_cols = slice(half * BANK, (half + 1) * BANK)
+                    scores = psum_scores.tile([P, BANK], F32, tag="scores")
+                    nc.tensor.matmul_mx(
+                        out=scores[:],
+                        lhsT=p_words[:, b_cols].bitcast(FP8X4),
+                        lhsT_scale=p_scales[:, b_cols],
+                        rhs=d2_words[:, r_cols].bitcast(FP8X4),
+                        rhs_scale=d2_scales[:, r_cols],
+                        start=True,
+                        stop=True,
+                    )
+                    nc.scalar.activation(out=result[:, r_cols], in_=scores[:], func=SIGMOID)
+                nc.sync.dma_start(out=out_rows[:, i * PAIR + j, :], in_=result[:])
+
+        for g in range(R_TILES // PAIR):
+            prepare_d2(g)
+
+        flipped = {}
+        products = {}
+        for step in range(ROUNDS + 2):
+            if step < ROUNDS:
+                flipped[step] = flip_inputs(step)
+            if 1 <= step <= ROUNDS:
+                products[step - 1] = first_product(*flipped[step - 1])
+            if step >= 2:
+                second_product(step - 2, *products[step - 2])

@@ -21,7 +21,7 @@ B_TILES = BATCH // P
 R_TILES = RELATIONS // P
 PAIR = 2
 ROUNDS = B_TILES // PAIR
-LOAD_TILES = 4
+D_PAIRS = R_TILES // PAIR
 WORDS = HIDDEN // 2
 
 FLOPS = 2 * BATCH * HIDDEN * HIDDEN + 2 * BATCH * HIDDEN * RELATIONS
@@ -34,9 +34,11 @@ def tile_dedicomdecoder_kernel(tc, z_i, z_j, R_words, R_scales, D, out):
         inputs = ctx.enter_context(tc.tile_pool(name="inputs", bufs=1))
         work = ctx.enter_context(tc.tile_pool(name="work", bufs=3))
         results = ctx.enter_context(tc.tile_pool(name="results", bufs=4))
-        psum_flip = ctx.enter_context(tc.psum_pool(name="psum_flip", bufs=2))
+        psum_zj = ctx.enter_context(tc.psum_pool(name="psum_zj", bufs=1))
+        psum_zi = ctx.enter_context(tc.psum_pool(name="psum_zi", bufs=1))
         psum_rz = ctx.enter_context(tc.psum_pool(name="psum_rz", bufs=2))
         psum_scores = ctx.enter_context(tc.psum_pool(name="psum_scores", bufs=4))
+        ctx.enter_context(tc.manual_schedule())
 
         zj_rows = z_j.rearrange("(p n) k -> p n k", n=B_TILES)
         zi_rows = z_i.rearrange("(p n) h -> p n h", n=B_TILES)
@@ -50,11 +52,21 @@ def tile_dedicomdecoder_kernel(tc, z_i, z_j, R_words, R_scales, D, out):
 
         ident_f32 = consts.tile([P, P], F32)
         ident_bf16 = consts.tile([P, P], BF16)
-        make_identity(nc, ident_bf16[:])
         make_identity(nc, ident_f32[:])
+        make_identity(nc, ident_bf16[:])
 
         w_words = consts.tile([P, HIDDEN], U32, align_bytes=64)
         w_scales = consts.tile([P, HIDDEN], U8, align_bytes=64)
+        d_in = [inputs.tile([P, PAIR * PAIR, HIDDEN], BF16, name="d_in%d" % c) for c in range(D_PAIRS // PAIR)]
+        zj_in = [inputs.tile([P, PAIR, HIDDEN], BF16, name="zj_in%d" % i) for i in range(ROUNDS)]
+        zi_in = [inputs.tile([P, PAIR, HIDDEN], BF16, name="zi_in%d" % i) for i in range(ROUNDS)]
+
+        def load_pair(tiles, rows, i):
+            nc.sync.dma_start(out=tiles[i][:], in_=rows[:, i * PAIR : (i + 1) * PAIR, :])
+
+        load_pair(zj_in, zj_rows, 0)
+        for c in range(D_PAIRS // PAIR):
+            nc.sync.dma_start(out=d_in[c][:], in_=d_rows[:, c * PAIR * PAIR : (c + 1) * PAIR * PAIR, :])
         nc.vector.memset(w_scales[:].bitcast(I32), 0)
         for r in range(4):
             nc.sync.dma_start(
@@ -63,39 +75,30 @@ def tile_dedicomdecoder_kernel(tc, z_i, z_j, R_words, R_scales, D, out):
         nc.sync.dma_start(
             out=w_words[:].bitcast(I32), in_=R_words[0].rearrange("p n t -> p (n t)").bitcast(I32)
         )
+        load_pair(zi_in, zi_rows, 0)
+        for i in range(1, ROUNDS):
+            load_pair(zj_in, zj_rows, i)
+            load_pair(zi_in, zi_rows, i)
 
-        d_in = [inputs.tile([P, LOAD_TILES, HIDDEN], BF16, name="d_in%d" % c) for c in range(R_TILES // LOAD_TILES)]
-        zj_in = [inputs.tile([P, LOAD_TILES, HIDDEN], BF16, name="zj_in%d" % c) for c in range(B_TILES // LOAD_TILES)]
-        zi_in = [inputs.tile([P, LOAD_TILES, HIDDEN], BF16, name="zi_in%d" % c) for c in range(B_TILES // LOAD_TILES)]
-
-        def load(tiles, rows, c):
-            nc.sync.dma_start(out=tiles[c][:], in_=rows[:, c * LOAD_TILES : (c + 1) * LOAD_TILES, :])
-
-        load(d_in, d_rows, 0)
-        load(zj_in, zj_rows, 0)
-        load(zi_in, zi_rows, 0)
-        load(d_in, d_rows, 1)
-        for c in range(1, B_TILES // LOAD_TILES):
-            load(zj_in, zj_rows, c)
-            load(zi_in, zi_rows, c)
-
-        d2_grouped = consts.tile([P, R_TILES // PAIR, PAIR, P, PACK], BF16, align_bytes=64)
+        d2_grouped = consts.tile([P, D_PAIRS, PAIR, P, PACK], BF16, align_bytes=64)
         d2_words = consts.tile([P, RELATIONS], U32, align_bytes=64)
         d2_scales = consts.tile([P, RELATIONS], U8, align_bytes=64)
 
-        def prepare_d2(g):
+        def square_d(g):
             d_flip = psum_scores.tile([P, PAIR, PACK, P], BF16, tag="scores")
             for j in range(PAIR):
                 n = g * PAIR + j
                 for t in range(PACK):
                     nc.tensor.transpose(
                         d_flip[:, j, t, :],
-                        d_in[n // LOAD_TILES][:, n % LOAD_TILES, t * P : (t + 1) * P],
+                        d_in[g // PAIR][:, n % (PAIR * PAIR), t * P : (t + 1) * P],
                         ident_bf16[:],
                     )
             nc.scalar.activation(
                 out=d2_grouped[:, g], in_=d_flip[:].rearrange("p j t r -> p j r t"), func=SQUARE
             )
+
+        def quantise_d2(g):
             cols = slice(g * PAIR * P, (g + 1) * PAIR * P)
             nc.vector.quantize_mx(
                 out=d2_words[:, cols].bitcast(FP8X4),
@@ -103,56 +106,60 @@ def tile_dedicomdecoder_kernel(tc, z_i, z_j, R_words, R_scales, D, out):
                 in_=d2_grouped[:, g].rearrange("p j r t -> p (j r t)"),
             )
 
-        def flip_inputs(i):
-            zj_flip = psum_flip.tile([P, PAIR, 2, P], F32, tag="flip")
+        def flip_zj(i):
+            zj_flip = psum_zj.tile([P, PAIR, 2, P], F32)
             for j in range(PAIR):
-                n = i * PAIR + j
-                words = zj_in[n // LOAD_TILES][:, n % LOAD_TILES, :].bitcast(F32)
+                words = zj_in[i][:, j, :].bitcast(F32)
                 for u in range(2):
                     nc.tensor.transpose(zj_flip[:, j, u, :], words[:, u:WORDS:2], ident_f32[:])
             zj_grouped = work.tile([P, PAIR * P * PACK], BF16, align_bytes=64)
-            nc.vector.tensor_copy(
+            nc.scalar.copy(
                 out=zj_grouped[:].bitcast(F32).rearrange("p (j b u) -> p j b u", j=PAIR, u=2),
                 in_=zj_flip[:].rearrange("p j u b -> p j b u"),
             )
-            zi_flip = psum_flip.tile([P, PAIR, PACK, P], BF16, tag="flip")
-            for j in range(PAIR):
-                n = i * PAIR + j
-                for t in range(PACK):
-                    nc.tensor.transpose(
-                        zi_flip[:, j, t, :],
-                        zi_in[n // LOAD_TILES][:, n % LOAD_TILES, t * P : (t + 1) * P],
-                        ident_bf16[:],
-                    )
-            zi_t = work.tile([P, PAIR, PACK, P], BF16)
-            nc.vector.tensor_copy(out=zi_t[:], in_=zi_flip[:])
+            return zj_grouped
+
+        def quantise_zj(zj_grouped):
             zj_words = work.tile([P, PAIR * P], U32, align_bytes=64)
             zj_scales = work.tile([P, PAIR * P], U8, align_bytes=64)
             nc.vector.quantize_mx(out=zj_words[:].bitcast(FP8X4), scales=zj_scales[:], in_=zj_grouped[:])
-            return zj_words, zj_scales, zi_t
+            return zj_words, zj_scales
 
-        def first_product(zj_words, zj_scales, zi_t):
-            p_grouped = work.tile([P, PAIR, P, PACK], BF16, align_bytes=64)
+        def flip_zi(i):
+            zi_flip = psum_zi.tile([P, PAIR, PACK, P], BF16)
             for j in range(PAIR):
-                b_cols = slice(j * P, (j + 1) * P)
-                rz = psum_rz.tile([P, PACK, P], F32)
                 for t in range(PACK):
-                    h_cols = slice(t * P, (t + 1) * P)
-                    nc.tensor.matmul_mx(
-                        out=rz[:, t, :],
-                        lhsT=w_words[:, h_cols].bitcast(FP8X4),
-                        lhsT_scale=w_scales[:, h_cols],
-                        rhs=zj_words[:, b_cols].bitcast(FP8X4),
-                        rhs_scale=zj_scales[:, b_cols],
-                        start=True,
-                        stop=True,
-                    )
-                nc.vector.tensor_tensor(
-                    out=p_grouped[:, j],
-                    in0=rz[:].rearrange("p t b -> p b t"),
-                    in1=zi_t[:, j].rearrange("p t b -> p b t"),
-                    op=MULT,
+                    nc.tensor.transpose(zi_flip[:, j, t, :], zi_in[i][:, j, t * P : (t + 1) * P], ident_bf16[:])
+            return zi_flip
+
+        def copy_zi(zi_flip):
+            zi_t = work.tile([P, PAIR, PACK, P], BF16)
+            nc.vector.tensor_copy(out=zi_t[:], in_=zi_flip[:])
+            return zi_t
+
+        def first_product(j, zj_q, zi_t, p_grouped):
+            zj_words, zj_scales = zj_q
+            b_cols = slice(j * P, (j + 1) * P)
+            rz = psum_rz.tile([P, PACK, P], F32)
+            for t in range(PACK):
+                h_cols = slice(t * P, (t + 1) * P)
+                nc.tensor.matmul_mx(
+                    out=rz[:, t, :],
+                    lhsT=w_words[:, h_cols].bitcast(FP8X4),
+                    lhsT_scale=w_scales[:, h_cols],
+                    rhs=zj_words[:, b_cols].bitcast(FP8X4),
+                    rhs_scale=zj_scales[:, b_cols],
+                    start=True,
+                    stop=True,
                 )
+            nc.vector.tensor_tensor(
+                out=p_grouped[:, j],
+                in0=rz[:].rearrange("p t b -> p b t"),
+                in1=zi_t[:, j].rearrange("p t b -> p b t"),
+                op=MULT,
+            )
+
+        def quantise_p(p_grouped):
             p_words = work.tile([P, PAIR * P], U32, align_bytes=64)
             p_scales = work.tile([P, PAIR * P], U8, align_bytes=64)
             nc.vector.quantize_mx(
@@ -162,7 +169,8 @@ def tile_dedicomdecoder_kernel(tc, z_i, z_j, R_words, R_scales, D, out):
             )
             return p_words, p_scales
 
-        def second_product(i, p_words, p_scales):
+        def second_product(i, p_q):
+            p_words, p_scales = p_q
             for j in range(PAIR):
                 b_cols = slice(j * P, (j + 1) * P)
                 result = results.tile([P, RELATIONS], F32)
@@ -181,15 +189,27 @@ def tile_dedicomdecoder_kernel(tc, z_i, z_j, R_words, R_scales, D, out):
                     nc.scalar.activation(out=result[:, r_cols], in_=scores[:], func=SIGMOID)
                 nc.sync.dma_start(out=out_rows[:, i * PAIR + j, :], in_=result[:])
 
-        for g in range(R_TILES // PAIR):
-            prepare_d2(g)
-
-        flipped = {}
-        products = {}
-        for step in range(ROUNDS + 2):
-            if step < ROUNDS:
-                flipped[step] = flip_inputs(step)
-            if 1 <= step <= ROUNDS:
-                products[step - 1] = first_product(*flipped[step - 1])
-            if step >= 2:
-                second_product(step - 2, *products[step - 2])
+        zj_q = {}
+        zi_t = {}
+        p_q = {}
+        for s in range(ROUNDS + 2):
+            if s < ROUNDS:
+                zj_grouped = flip_zj(s)
+                if s == 0:
+                    for g in range(D_PAIRS):
+                        square_d(g)
+                zi_flip = flip_zi(s)
+            if 1 <= s <= ROUNDS:
+                p_grouped = work.tile([P, PAIR, P, PACK], BF16, align_bytes=64)
+                first_product(0, zj_q[s - 1], zi_t[s - 1], p_grouped)
+            if s < ROUNDS:
+                zi_t[s] = copy_zi(zi_flip)
+                zj_q[s] = quantise_zj(zj_grouped)
+            if 1 <= s <= ROUNDS:
+                first_product(1, zj_q[s - 1], zi_t[s - 1], p_grouped)
+                p_q[s - 1] = quantise_p(p_grouped)
+            if s == 0:
+                for g in range(D_PAIRS):
+                    quantise_d2(g)
+            if s >= 2:
+                second_product(s - 2, p_q[s - 2])

@@ -23,6 +23,8 @@ PAIR = 2
 ROUNDS = B_TILES // PAIR
 D_PAIRS = R_TILES // PAIR
 WORDS = HIDDEN // 2
+WARM_UP = 4
+WARM_STEPS = 2
 
 FLOPS = 2 * BATCH * HIDDEN * HIDDEN + 2 * BATCH * HIDDEN * RELATIONS
 
@@ -44,6 +46,16 @@ def tile_dedicomdecoder_kernel(tc, z_i, z_j, R_words, R_scales, D, out):
         zi_rows = z_i.rearrange("(p n) h -> p n h", n=B_TILES)
         out_rows = out.rearrange("(p n) r -> p n r", n=B_TILES)
         d_rows = D.rearrange("(n p) h -> p n h", p=P)
+
+        zeros = consts.tile([P, BANK], BF16)
+        nc.vector.memset(zeros[:], 0.0)
+        unread = psum_rz.tile([P, BANK], F32, tag="rz")
+
+        def matmuls_on_zeros(count):
+            for k in range(count):
+                nc.tensor.matmul(out=unread[:], lhsT=zeros[:, :P], rhs=zeros[:], start=True, stop=True)
+
+        matmuls_on_zeros(WARM_UP)
 
         warm_in = consts.tile([P, 1], F32)
         warm_out = consts.tile([P, 1], F32)
@@ -94,6 +106,7 @@ def tile_dedicomdecoder_kernel(tc, z_i, z_j, R_words, R_scales, D, out):
                         d_in[g // PAIR][:, n % (PAIR * PAIR), t * P : (t + 1) * P],
                         ident_bf16[:],
                     )
+            matmuls_on_zeros(1)
             nc.scalar.activation(
                 out=d2_grouped[:, g], in_=d_flip[:].rearrange("p j t r -> p j r t"), func=SQUARE
             )
@@ -112,6 +125,8 @@ def tile_dedicomdecoder_kernel(tc, z_i, z_j, R_words, R_scales, D, out):
                 words = zj_in[i][:, j, :].bitcast(F32)
                 for u in range(2):
                     nc.tensor.transpose(zj_flip[:, j, u, :], words[:, u:WORDS:2], ident_f32[:])
+            if i < WARM_STEPS:
+                matmuls_on_zeros(1)
             zj_grouped = work.tile([P, PAIR * P * PACK], BF16, align_bytes=64)
             nc.scalar.copy(
                 out=zj_grouped[:].bitcast(F32).rearrange("p (j b u) -> p j b u", j=PAIR, u=2),
@@ -130,6 +145,8 @@ def tile_dedicomdecoder_kernel(tc, z_i, z_j, R_words, R_scales, D, out):
             for j in range(PAIR):
                 for t in range(PACK):
                     nc.tensor.transpose(zi_flip[:, j, t, :], zi_in[i][:, j, t * P : (t + 1) * P], ident_bf16[:])
+            if i < WARM_STEPS:
+                matmuls_on_zeros(1)
             return zi_flip
 
         def copy_zi(zi_flip):
@@ -140,7 +157,7 @@ def tile_dedicomdecoder_kernel(tc, z_i, z_j, R_words, R_scales, D, out):
         def first_product(j, zj_q, zi_t, p_grouped):
             zj_words, zj_scales = zj_q
             b_cols = slice(j * P, (j + 1) * P)
-            rz = psum_rz.tile([P, PACK, P], F32)
+            rz = psum_rz.tile([P, PACK, P], F32, tag="rz")
             for t in range(PACK):
                 h_cols = slice(t * P, (t + 1) * P)
                 nc.tensor.matmul_mx(

@@ -35,7 +35,7 @@ def tile_dedicomdecoder_kernel(tc, z_i, z_j, R_words, R_scales, D, out):
         consts = ctx.enter_context(tc.tile_pool(name="consts", bufs=1))
         inputs = ctx.enter_context(tc.tile_pool(name="inputs", bufs=1))
         work = ctx.enter_context(tc.tile_pool(name="work", bufs=3))
-        results = ctx.enter_context(tc.tile_pool(name="results", bufs=4))
+        results = ctx.enter_context(tc.tile_pool(name="results", bufs=8))
         psum_zj = ctx.enter_context(tc.psum_pool(name="psum_zj", bufs=1))
         psum_zi = ctx.enter_context(tc.psum_pool(name="psum_zi", bufs=1))
         psum_rz = ctx.enter_context(tc.psum_pool(name="psum_rz", bufs=2))
@@ -190,7 +190,6 @@ def tile_dedicomdecoder_kernel(tc, z_i, z_j, R_words, R_scales, D, out):
             p_words, p_scales = p_q
             for j in range(PAIR):
                 b_cols = slice(j * P, (j + 1) * P)
-                result = results.tile([P, RELATIONS], F32)
                 for half in range(RELATIONS // BANK):
                     r_cols = slice(half * BANK, (half + 1) * BANK)
                     scores = psum_scores.tile([P, BANK], F32, tag="scores")
@@ -203,8 +202,9 @@ def tile_dedicomdecoder_kernel(tc, z_i, z_j, R_words, R_scales, D, out):
                         start=True,
                         stop=True,
                     )
-                    nc.scalar.activation(out=result[:, r_cols], in_=scores[:], func=SIGMOID)
-                nc.sync.dma_start(out=out_rows[:, i * PAIR + j, :], in_=result[:])
+                    result = results.tile([P, BANK], F32)
+                    nc.scalar.activation(out=result[:], in_=scores[:], func=SIGMOID)
+                    nc.sync.dma_start(out=out_rows[:, i * PAIR + j, r_cols], in_=result[:])
 
         zj_q = {}
         zi_t = {}
@@ -215,12 +215,11 @@ def tile_dedicomdecoder_kernel(tc, z_i, z_j, R_words, R_scales, D, out):
                 if s == 0:
                     for g in range(D_PAIRS):
                         square_d(g)
-                zi_flip = flip_zi(s)
+                zi_t[s] = copy_zi(flip_zi(s))
             if 1 <= s <= ROUNDS:
                 p_grouped = work.tile([P, PAIR, P, PACK], BF16, align_bytes=64)
                 first_product(0, zj_q[s - 1], zi_t[s - 1], p_grouped)
             if s < ROUNDS:
-                zi_t[s] = copy_zi(zi_flip)
                 zj_q[s] = quantise_zj(zj_grouped)
             if 1 <= s <= ROUNDS:
                 first_product(1, zj_q[s - 1], zi_t[s - 1], p_grouped)

@@ -23,6 +23,8 @@ PAIR = 2
 ROUNDS = B_TILES // PAIR
 D_PAIRS = R_TILES // PAIR
 WORDS = HIDDEN // 2
+LOAD_GROUPS = ((0, 1), (1, 2), (2, 4), (4, 8))
+FINE_ROUNDS = 3
 WARM_UP = 4
 WARM_STEPS = 2
 
@@ -35,7 +37,7 @@ def tile_dedicomdecoder_kernel(tc, z_i, z_j, R_words, R_scales, D, out):
         consts = ctx.enter_context(tc.tile_pool(name="consts", bufs=1))
         inputs = ctx.enter_context(tc.tile_pool(name="inputs", bufs=1))
         work = ctx.enter_context(tc.tile_pool(name="work", bufs=3))
-        results = ctx.enter_context(tc.tile_pool(name="results", bufs=8))
+        results = ctx.enter_context(tc.tile_pool(name="results", bufs=3))
         psum_zj = ctx.enter_context(tc.psum_pool(name="psum_zj", bufs=1))
         psum_zi = ctx.enter_context(tc.psum_pool(name="psum_zi", bufs=1))
         psum_rz = ctx.enter_context(tc.psum_pool(name="psum_rz", bufs=2))
@@ -70,13 +72,22 @@ def tile_dedicomdecoder_kernel(tc, z_i, z_j, R_words, R_scales, D, out):
         w_words = consts.tile([P, HIDDEN], U32, align_bytes=64)
         w_scales = consts.tile([P, HIDDEN], U8, align_bytes=64)
         d_in = [inputs.tile([P, PAIR * PAIR, HIDDEN], BF16, name="d_in%d" % c) for c in range(D_PAIRS // PAIR)]
-        zj_in = [inputs.tile([P, PAIR, HIDDEN], BF16, name="zj_in%d" % i) for i in range(ROUNDS)]
-        zi_in = [inputs.tile([P, PAIR, HIDDEN], BF16, name="zi_in%d" % i) for i in range(ROUNDS)]
+        zj_loaded = [
+            inputs.tile([P, (b - a) * PAIR, HIDDEN], BF16, name="zj_loaded%d" % a) for a, b in LOAD_GROUPS
+        ]
+        zi_loaded = [
+            inputs.tile([P, (b - a) * PAIR, HIDDEN], BF16, name="zi_loaded%d" % a) for a, b in LOAD_GROUPS
+        ]
 
-        def load_pair(tiles, rows, i):
-            nc.sync.dma_start(out=tiles[i][:], in_=rows[:, i * PAIR : (i + 1) * PAIR, :])
+        def load_group(tiles, rows, c):
+            a, b = LOAD_GROUPS[c]
+            nc.sync.dma_start(out=tiles[c][:], in_=rows[:, a * PAIR : b * PAIR, :])
 
-        load_pair(zj_in, zj_rows, 0)
+        def batch_tile(tiles, i, j):
+            c = [a <= i < b for a, b in LOAD_GROUPS].index(True)
+            return tiles[c][:, (i - LOAD_GROUPS[c][0]) * PAIR + j, :]
+
+        load_group(zj_loaded, zj_rows, 0)
         for c in range(D_PAIRS // PAIR):
             nc.sync.dma_start(out=d_in[c][:], in_=d_rows[:, c * PAIR * PAIR : (c + 1) * PAIR * PAIR, :])
         nc.vector.memset(w_scales[:].bitcast(I32), 0)
@@ -87,10 +98,10 @@ def tile_dedicomdecoder_kernel(tc, z_i, z_j, R_words, R_scales, D, out):
         nc.sync.dma_start(
             out=w_words[:].bitcast(I32), in_=R_words[0].rearrange("p n t -> p (n t)").bitcast(I32)
         )
-        load_pair(zi_in, zi_rows, 0)
-        for i in range(1, ROUNDS):
-            load_pair(zj_in, zj_rows, i)
-            load_pair(zi_in, zi_rows, i)
+        load_group(zi_loaded, zi_rows, 0)
+        for c in range(1, len(LOAD_GROUPS)):
+            load_group(zj_loaded, zj_rows, c)
+            load_group(zi_loaded, zi_rows, c)
 
         d2_grouped = consts.tile([P, D_PAIRS, PAIR, P, PACK], BF16, align_bytes=64)
         d2_words = consts.tile([P, RELATIONS], U32, align_bytes=64)
@@ -122,7 +133,7 @@ def tile_dedicomdecoder_kernel(tc, z_i, z_j, R_words, R_scales, D, out):
         def flip_zj(i):
             zj_flip = psum_zj.tile([P, PAIR, 2, P], F32)
             for j in range(PAIR):
-                words = zj_in[i][:, j, :].bitcast(F32)
+                words = batch_tile(zj_loaded, i, j).bitcast(F32)
                 for u in range(2):
                     nc.tensor.transpose(zj_flip[:, j, u, :], words[:, u:WORDS:2], ident_f32[:])
             if i < WARM_STEPS:
@@ -144,7 +155,9 @@ def tile_dedicomdecoder_kernel(tc, z_i, z_j, R_words, R_scales, D, out):
             zi_flip = psum_zi.tile([P, PAIR, PACK, P], BF16)
             for j in range(PAIR):
                 for t in range(PACK):
-                    nc.tensor.transpose(zi_flip[:, j, t, :], zi_in[i][:, j, t * P : (t + 1) * P], ident_bf16[:])
+                    nc.tensor.transpose(
+                        zi_flip[:, j, t, :], batch_tile(zi_loaded, i, j)[:, t * P : (t + 1) * P], ident_bf16[:]
+                    )
             if i < WARM_STEPS:
                 matmuls_on_zeros(1)
             return zi_flip
@@ -188,6 +201,7 @@ def tile_dedicomdecoder_kernel(tc, z_i, z_j, R_words, R_scales, D, out):
 
         def second_product(i, p_q):
             p_words, p_scales = p_q
+            result = results.tile([P, PAIR, RELATIONS], F32)
             for j in range(PAIR):
                 b_cols = slice(j * P, (j + 1) * P)
                 for half in range(RELATIONS // BANK):
@@ -202,9 +216,11 @@ def tile_dedicomdecoder_kernel(tc, z_i, z_j, R_words, R_scales, D, out):
                         start=True,
                         stop=True,
                     )
-                    result = results.tile([P, BANK], F32)
-                    nc.scalar.activation(out=result[:], in_=scores[:], func=SIGMOID)
-                    nc.sync.dma_start(out=out_rows[:, i * PAIR + j, r_cols], in_=result[:])
+                    nc.scalar.activation(out=result[:, j, r_cols], in_=scores[:], func=SIGMOID)
+                    if i >= ROUNDS - FINE_ROUNDS:
+                        nc.sync.dma_start(out=out_rows[:, i * PAIR + j, r_cols], in_=result[:, j, r_cols])
+                if i < ROUNDS - FINE_ROUNDS:
+                    nc.sync.dma_start(out=out_rows[:, i * PAIR + j, :], in_=result[:, j, :])
 
         zj_q = {}
         zi_t = {}

@@ -23,8 +23,10 @@ PAIR = 2
 ROUNDS = B_TILES // PAIR
 D_PAIRS = R_TILES // PAIR
 WORDS = HIDDEN // 2
-LOAD_GROUPS = ((0, 1), (1, 2), (2, 4), (4, 8))
+HALVES = WORDS // P
+LOAD_GROUPS = ((0, 1), (1, 2), (2, 3), (3, 4), (4, 8))
 FINE_ROUNDS = 3
+D_STEPS = ((0, 1), (2,), (3,))
 WARM_UP = 4
 WARM_STEPS = 2
 
@@ -37,9 +39,9 @@ def tile_dedicomdecoder_kernel(tc, z_i, z_j, R_words, R_scales, D, out):
         consts = ctx.enter_context(tc.tile_pool(name="consts", bufs=1))
         inputs = ctx.enter_context(tc.tile_pool(name="inputs", bufs=1))
         work = ctx.enter_context(tc.tile_pool(name="work", bufs=3))
-        results = ctx.enter_context(tc.tile_pool(name="results", bufs=3))
+        results = ctx.enter_context(tc.tile_pool(name="results", bufs=6))
         psum_zj = ctx.enter_context(tc.psum_pool(name="psum_zj", bufs=1))
-        psum_zi = ctx.enter_context(tc.psum_pool(name="psum_zi", bufs=1))
+        psum_p = ctx.enter_context(tc.psum_pool(name="psum_p", bufs=1))
         psum_rz = ctx.enter_context(tc.psum_pool(name="psum_rz", bufs=2))
         psum_scores = ctx.enter_context(tc.psum_pool(name="psum_scores", bufs=4))
         ctx.enter_context(tc.manual_schedule())
@@ -51,7 +53,7 @@ def tile_dedicomdecoder_kernel(tc, z_i, z_j, R_words, R_scales, D, out):
 
         zeros = consts.tile([P, BANK], BF16)
         nc.vector.memset(zeros[:], 0.0)
-        unread = psum_rz.tile([P, BANK], F32, tag="rz")
+        unread = psum_p.tile([P, BANK], F32, tag="p_flip")
 
         def matmuls_on_zeros(count):
             for k in range(count):
@@ -64,146 +66,120 @@ def tile_dedicomdecoder_kernel(tc, z_i, z_j, R_words, R_scales, D, out):
         nc.vector.memset(warm_in[:], 0.0)
         nc.scalar.activation(out=warm_out[:], in_=warm_in[:], func=SIGMOID)
 
-        ident_f32 = consts.tile([P, P], F32)
-        ident_bf16 = consts.tile([P, P], BF16)
-        make_identity(nc, ident_f32[:])
-        make_identity(nc, ident_bf16[:])
+        ident = consts.tile([P, P], F32)
+        make_identity(nc, ident[:])
 
         w_words = consts.tile([P, HIDDEN], U32, align_bytes=64)
         w_scales = consts.tile([P, HIDDEN], U8, align_bytes=64)
-        d_in = [inputs.tile([P, PAIR * PAIR, HIDDEN], BF16, name="d_in%d" % c) for c in range(D_PAIRS // PAIR)]
-        zj_loaded = [
-            inputs.tile([P, (b - a) * PAIR, HIDDEN], BF16, name="zj_loaded%d" % a) for a, b in LOAD_GROUPS
-        ]
-        zi_loaded = [
-            inputs.tile([P, (b - a) * PAIR, HIDDEN], BF16, name="zi_loaded%d" % a) for a, b in LOAD_GROUPS
-        ]
+        d_in = [inputs.tile([P, PAIR, HIDDEN], BF16, name="d_in%d" % g) for g in range(D_PAIRS)]
+        zj_in = {a: inputs.tile([P, (b - a) * PAIR, HIDDEN], BF16, name="zj_in%d" % a) for a, b in LOAD_GROUPS}
+        zi_in = {a: inputs.tile([P, (b - a) * PAIR, HIDDEN], BF16, name="zi_in%d" % a) for a, b in LOAD_GROUPS}
 
-        def load_group(tiles, rows, c):
-            a, b = LOAD_GROUPS[c]
-            nc.sync.dma_start(out=tiles[c][:], in_=rows[:, a * PAIR : b * PAIR, :])
+        def load_rounds(tiles, rows, a):
+            if a in tiles:
+                count = tiles[a][:].shape[1]
+                nc.sync.dma_start(out=tiles[a][:], in_=rows[:, a * PAIR : a * PAIR + count, :])
 
-        def batch_tile(tiles, i, j):
-            c = [a <= i < b for a, b in LOAD_GROUPS].index(True)
-            return tiles[c][:, (i - LOAD_GROUPS[c][0]) * PAIR + j, :]
+        def pair_of(tiles, i):
+            a = max(first for first in tiles if first <= i)
+            return tiles[a][:, (i - a) * PAIR : (i - a + 1) * PAIR, :]
 
-        load_group(zj_loaded, zj_rows, 0)
-        for c in range(D_PAIRS // PAIR):
-            nc.sync.dma_start(out=d_in[c][:], in_=d_rows[:, c * PAIR * PAIR : (c + 1) * PAIR * PAIR, :])
-        nc.vector.memset(w_scales[:].bitcast(I32), 0)
-        for r in range(4):
+        def load_w():
+            for r in range(4):
+                nc.sync.dma_start(
+                    out=w_scales[:].bitcast(I32)[r:P:32, :], in_=R_scales[0].bitcast(I32)[r:16:4, :]
+                )
             nc.sync.dma_start(
-                out=w_scales[:].bitcast(I32)[r:P:32, :], in_=R_scales[0].bitcast(I32)[r:16:4, :]
+                out=w_words[:].bitcast(I32), in_=R_words[0].rearrange("p n t -> p (n t)").bitcast(I32)
             )
-        nc.sync.dma_start(
-            out=w_words[:].bitcast(I32), in_=R_words[0].rearrange("p n t -> p (n t)").bitcast(I32)
-        )
-        load_group(zi_loaded, zi_rows, 0)
-        for c in range(1, len(LOAD_GROUPS)):
-            load_group(zj_loaded, zj_rows, c)
-            load_group(zi_loaded, zi_rows, c)
 
-        d2_grouped = consts.tile([P, D_PAIRS, PAIR, P, PACK], BF16, align_bytes=64)
+        nc.vector.memset(w_scales[:].bitcast(I32), 0)
+        for s in range(ROUNDS + 1):
+            load_rounds(zj_in, zj_rows, s)
+            if s == 1:
+                load_w()
+            if s < len(D_STEPS):
+                for g in D_STEPS[s]:
+                    nc.sync.dma_start(out=d_in[g][:], in_=d_rows[:, g * PAIR : (g + 1) * PAIR, :])
+            load_rounds(zi_in, zi_rows, s - 1)
+
+        def flip_words(flipped, rows, step):
+            for j in range(PAIR):
+                words = rows[:, j, :].bitcast(F32)
+                for u in range(HALVES):
+                    picked = words[:, u:WORDS:2] if step == 2 else words[:, u * P : (u + 1) * P]
+                    nc.tensor.transpose(flipped[:, u, j * P : (j + 1) * P], picked, ident[:])
+
+        def regroup(engine_copy, grouped, flipped):
+            engine_copy(
+                out=grouped.bitcast(F32).rearrange("p (n u) -> p n u", u=HALVES),
+                in_=flipped[:].rearrange("p u n -> p n u"),
+            )
+
+        d2_grouped = consts.tile([P, D_PAIRS, PAIR * P * PACK], BF16, align_bytes=64)
         d2_words = consts.tile([P, RELATIONS], U32, align_bytes=64)
         d2_scales = consts.tile([P, RELATIONS], U8, align_bytes=64)
 
-        def square_d(g):
-            d_flip = psum_scores.tile([P, PAIR, PACK, P], BF16, tag="scores")
-            for j in range(PAIR):
-                n = g * PAIR + j
-                for t in range(PACK):
-                    nc.tensor.transpose(
-                        d_flip[:, j, t, :],
-                        d_in[g // PAIR][:, n % (PAIR * PAIR), t * P : (t + 1) * P],
-                        ident_bf16[:],
-                    )
-            matmuls_on_zeros(1)
+        def square_d(g, s):
+            d_flip = psum_scores.tile([P, HALVES, PAIR * P], F32, tag="scores")
+            flip_words(d_flip, d_in[g][:], 1)
+            if s < WARM_STEPS:
+                matmuls_on_zeros(1)
             nc.scalar.activation(
-                out=d2_grouped[:, g], in_=d_flip[:].rearrange("p j t r -> p j r t"), func=SQUARE
+                out=d2_grouped[:, g].rearrange("p (n u e) -> p n u e", u=HALVES, e=2),
+                in_=d_flip[:].rearrange("p u n -> p (u n)").bitcast(BF16).rearrange("p (u n e) -> p n u e", u=HALVES, e=2),
+                func=SQUARE,
             )
 
         def quantise_d2(g):
             cols = slice(g * PAIR * P, (g + 1) * PAIR * P)
-            nc.vector.quantize_mx(
-                out=d2_words[:, cols].bitcast(FP8X4),
-                scales=d2_scales[:, cols],
-                in_=d2_grouped[:, g].rearrange("p j r t -> p (j r t)"),
-            )
+            nc.vector.quantize_mx(out=d2_words[:, cols].bitcast(FP8X4), scales=d2_scales[:, cols], in_=d2_grouped[:, g])
 
         def flip_zj(i):
-            zj_flip = psum_zj.tile([P, PAIR, 2, P], F32)
-            for j in range(PAIR):
-                words = batch_tile(zj_loaded, i, j).bitcast(F32)
-                for u in range(2):
-                    nc.tensor.transpose(zj_flip[:, j, u, :], words[:, u:WORDS:2], ident_f32[:])
+            zj_flip = psum_zj.tile([P, HALVES, PAIR * P], F32)
+            flip_words(zj_flip, pair_of(zj_in, i), 2)
             if i < WARM_STEPS:
                 matmuls_on_zeros(1)
             zj_grouped = work.tile([P, PAIR * P * PACK], BF16, align_bytes=64)
-            nc.scalar.copy(
-                out=zj_grouped[:].bitcast(F32).rearrange("p (j b u) -> p j b u", j=PAIR, u=2),
-                in_=zj_flip[:].rearrange("p j u b -> p j b u"),
-            )
+            regroup(nc.scalar.copy, zj_grouped[:], zj_flip)
             return zj_grouped
 
-        def quantise_zj(zj_grouped):
-            zj_words = work.tile([P, PAIR * P], U32, align_bytes=64)
-            zj_scales = work.tile([P, PAIR * P], U8, align_bytes=64)
-            nc.vector.quantize_mx(out=zj_words[:].bitcast(FP8X4), scales=zj_scales[:], in_=zj_grouped[:])
-            return zj_words, zj_scales
+        def quantise(label, grouped):
+            words = work.tile([P, PAIR * P], U32, name=label + "_words", align_bytes=64)
+            scales = work.tile([P, PAIR * P], U8, name=label + "_scales", align_bytes=64)
+            nc.vector.quantize_mx(out=words[:].bitcast(FP8X4), scales=scales[:], in_=grouped[:])
+            return words, scales
 
-        def flip_zi(i):
-            zi_flip = psum_zi.tile([P, PAIR, PACK, P], BF16)
-            for j in range(PAIR):
-                for t in range(PACK):
-                    nc.tensor.transpose(
-                        zi_flip[:, j, t, :], batch_tile(zi_loaded, i, j)[:, t * P : (t + 1) * P], ident_bf16[:]
-                    )
-            if i < WARM_STEPS:
-                matmuls_on_zeros(1)
-            return zi_flip
-
-        def copy_zi(zi_flip):
-            zi_t = work.tile([P, PAIR, PACK, P], BF16)
-            nc.vector.tensor_copy(out=zi_t[:], in_=zi_flip[:])
-            return zi_t
-
-        def first_product(j, zj_q, zi_t, p_grouped):
+        def first_product(j, zj_q):
             zj_words, zj_scales = zj_q
             b_cols = slice(j * P, (j + 1) * P)
-            rz = psum_rz.tile([P, PACK, P], F32, tag="rz")
-            for t in range(PACK):
-                h_cols = slice(t * P, (t + 1) * P)
-                nc.tensor.matmul_mx(
-                    out=rz[:, t, :],
-                    lhsT=w_words[:, h_cols].bitcast(FP8X4),
-                    lhsT_scale=w_scales[:, h_cols],
-                    rhs=zj_words[:, b_cols].bitcast(FP8X4),
-                    rhs_scale=zj_scales[:, b_cols],
-                    start=True,
-                    stop=True,
-                )
-            nc.vector.tensor_tensor(
-                out=p_grouped[:, j],
-                in0=rz[:].rearrange("p t b -> p b t"),
-                in1=zi_t[:, j].rearrange("p t b -> p b t"),
-                op=MULT,
+            rz = psum_rz.tile([P, HIDDEN], F32)
+            nc.tensor.matmul_mx(
+                out=rz[:],
+                lhsT=zj_words[:, b_cols].bitcast(FP8X4),
+                lhsT_scale=zj_scales[:, b_cols],
+                rhs=w_words[:].bitcast(FP8X4),
+                rhs_scale=w_scales[:],
+                start=True,
+                stop=True,
             )
+            return rz
 
-        def quantise_p(p_grouped):
-            p_words = work.tile([P, PAIR * P], U32, align_bytes=64)
-            p_scales = work.tile([P, PAIR * P], U8, align_bytes=64)
-            nc.vector.quantize_mx(
-                out=p_words[:].bitcast(FP8X4),
-                scales=p_scales[:],
-                in_=p_grouped[:].rearrange("p j b t -> p (j b t)"),
-            )
-            return p_words, p_scales
+        def times_zi(i, j, rz, p_rows):
+            nc.vector.tensor_tensor(out=p_rows[:, j, :], in0=rz[:], in1=pair_of(zi_in, i)[:, j, :], op=MULT)
+
+        def flip_p(i, p_rows):
+            p_flip = psum_p.tile([P, HALVES, PAIR * P], F32)
+            flip_words(p_flip, p_rows[:], 1)
+            p_grouped = work.tile([P, PAIR * P * PACK], BF16, align_bytes=64)
+            regroup(nc.scalar.copy if i == 0 else nc.vector.tensor_copy, p_grouped[:], p_flip)
+            return p_grouped
 
         def second_product(i, p_q):
             p_words, p_scales = p_q
-            result = results.tile([P, PAIR, RELATIONS], F32)
             for j in range(PAIR):
                 b_cols = slice(j * P, (j + 1) * P)
+                result = results.tile([P, RELATIONS], F32)
                 for half in range(RELATIONS // BANK):
                     r_cols = slice(half * BANK, (half + 1) * BANK)
                     scores = psum_scores.tile([P, BANK], F32, tag="scores")
@@ -216,32 +192,34 @@ def tile_dedicomdecoder_kernel(tc, z_i, z_j, R_words, R_scales, D, out):
                         start=True,
                         stop=True,
                     )
-                    nc.scalar.activation(out=result[:, j, r_cols], in_=scores[:], func=SIGMOID)
+                    nc.scalar.activation(out=result[:, r_cols], in_=scores[:], func=SIGMOID)
                     if i >= ROUNDS - FINE_ROUNDS:
-                        nc.sync.dma_start(out=out_rows[:, i * PAIR + j, r_cols], in_=result[:, j, r_cols])
+                        nc.sync.dma_start(out=out_rows[:, i * PAIR + j, r_cols], in_=result[:, r_cols])
                 if i < ROUNDS - FINE_ROUNDS:
-                    nc.sync.dma_start(out=out_rows[:, i * PAIR + j, :], in_=result[:, j, :])
+                    nc.sync.dma_start(out=out_rows[:, i * PAIR + j, :], in_=result[:])
 
         zj_q = {}
-        zi_t = {}
+        p_rows = {}
         p_q = {}
-        for s in range(ROUNDS + 2):
+        for s in range(ROUNDS + 3):
+            d_pairs = D_STEPS[s] if s < len(D_STEPS) else ()
             if s < ROUNDS:
                 zj_grouped = flip_zj(s)
-                if s == 0:
-                    for g in range(D_PAIRS):
-                        square_d(g)
-                zi_t[s] = copy_zi(flip_zi(s))
-            if 1 <= s <= ROUNDS:
-                p_grouped = work.tile([P, PAIR, P, PACK], BF16, align_bytes=64)
-                first_product(0, zj_q[s - 1], zi_t[s - 1], p_grouped)
+            for g in d_pairs:
+                square_d(g, s)
+            if 0 <= s - 2 < ROUNDS:
+                p_grouped = flip_p(s - 2, p_rows[s - 2])
+            if 0 <= s - 1 < ROUNDS:
+                rz = [first_product(j, zj_q[s - 1]) for j in range(PAIR)]
+                p_rows[s - 1] = work.tile([P, PAIR, HIDDEN], BF16, name="p_rows")
+                times_zi(s - 1, 0, rz[0], p_rows[s - 1])
             if s < ROUNDS:
-                zj_q[s] = quantise_zj(zj_grouped)
-            if 1 <= s <= ROUNDS:
-                first_product(1, zj_q[s - 1], zi_t[s - 1], p_grouped)
-                p_q[s - 1] = quantise_p(p_grouped)
-            if s == 0:
-                for g in range(D_PAIRS):
-                    quantise_d2(g)
-            if s >= 2:
-                second_product(s - 2, p_q[s - 2])
+                zj_q[s] = quantise("zj", zj_grouped)
+            if 0 <= s - 1 < ROUNDS:
+                times_zi(s - 1, 1, rz[1], p_rows[s - 1])
+            if 0 <= s - 2 < ROUNDS:
+                p_q[s - 2] = quantise("p", p_grouped)
+            for g in d_pairs:
+                quantise_d2(g)
+            if s >= 3:
+                second_product(s - 3, p_q[s - 3])

@@ -38,8 +38,8 @@ def tile_dedicomdecoder_kernel(tc, z_i, z_j, R_words, R_scales, D, out):
     with ExitStack() as ctx:
         consts = ctx.enter_context(tc.tile_pool(name="consts", bufs=1))
         inputs = ctx.enter_context(tc.tile_pool(name="inputs", bufs=1))
-        work = ctx.enter_context(tc.tile_pool(name="work", bufs=3))
-        results = ctx.enter_context(tc.tile_pool(name="results", bufs=6))
+        work = ctx.enter_context(tc.tile_pool(name="work", bufs=ROUNDS))
+        results = ctx.enter_context(tc.tile_pool(name="results", bufs=B_TILES))
         psum_zj = ctx.enter_context(tc.psum_pool(name="psum_zj", bufs=1))
         psum_p = ctx.enter_context(tc.psum_pool(name="psum_p", bufs=1))
         psum_rz = ctx.enter_context(tc.psum_pool(name="psum_rz", bufs=2))

@@ -120,16 +120,24 @@ def tile_dedicomdecoder_kernel(tc, z_i, z_j, R_words, R_scales, D, out):
         d2_words = consts.tile([P, RELATIONS], U32, align_bytes=64)
         d2_scales = consts.tile([P, RELATIONS], U8, align_bytes=64)
 
-        def square_d(g, s):
+        def square_rows(g):
+            d2_rows = inputs.tile([P, PAIR, HIDDEN], BF16, name="d2_rows%d" % g)
+            nc.vector.tensor_tensor(out=d2_rows[:], in0=d_in[g][:], in1=d_in[g][:], op=MULT)
+            return d2_rows
+
+        def flip_d(g, s, d2_rows):
             d_flip = psum_scores.tile([P, HALVES, PAIR * P], F32, tag="scores")
-            flip_words(d_flip, d_in[g][:], 1)
+            flip_words(d_flip, d_in[g][:] if d2_rows is None else d2_rows[:], 1)
             if s < WARM_STEPS:
                 matmuls_on_zeros(1)
-            nc.scalar.activation(
-                out=d2_grouped[:, g].rearrange("p (n u e) -> p n u e", u=HALVES, e=2),
-                in_=d_flip[:].rearrange("p u n -> p (u n)").bitcast(BF16).rearrange("p (u n e) -> p n u e", u=HALVES, e=2),
-                func=SQUARE,
-            )
+            if d2_rows is None:
+                nc.scalar.activation(
+                    out=d2_grouped[:, g].rearrange("p (n u e) -> p n u e", u=HALVES, e=2),
+                    in_=d_flip[:].rearrange("p u n -> p (u n)").bitcast(BF16).rearrange("p (u n e) -> p n u e", u=HALVES, e=2),
+                    func=SQUARE,
+                )
+            else:
+                regroup(nc.scalar.copy, d2_grouped[:, g], d_flip)
 
         def quantise_d2(g):
             cols = slice(g * PAIR * P, (g + 1) * PAIR * P)
@@ -203,14 +211,16 @@ def tile_dedicomdecoder_kernel(tc, z_i, z_j, R_words, R_scales, D, out):
         p_q = {}
         for s in range(ROUNDS + 3):
             d_pairs = D_STEPS[s] if s < len(D_STEPS) else ()
+            d2_rows = {g: square_rows(g) if s == 0 else None for g in d_pairs}
             if s < ROUNDS:
                 zj_grouped = flip_zj(s)
-            for g in d_pairs:
-                square_d(g, s)
             if 0 <= s - 2 < ROUNDS:
                 p_grouped = flip_p(s - 2, p_rows[s - 2])
             if 0 <= s - 1 < ROUNDS:
                 rz = [first_product(j, zj_q[s - 1]) for j in range(PAIR)]
+            for g in d_pairs:
+                flip_d(g, s, d2_rows[g])
+            if 0 <= s - 1 < ROUNDS:
                 p_rows[s - 1] = work.tile([P, PAIR, HIDDEN], BF16, name="p_rows")
                 times_zi(s - 1, 0, rz[0], p_rows[s - 1])
             if s < ROUNDS:

@@ -222,11 +222,10 @@ def tile_dedicomdecoder_kernel(tc, z_i, z_j, R_words, R_scales, D, out):
                 flip_d(g, s, d2_rows[g])
             if 0 <= s - 1 < ROUNDS:
                 p_rows[s - 1] = work.tile([P, PAIR, HIDDEN], BF16, name="p_rows")
-                times_zi(s - 1, 0, rz[0], p_rows[s - 1])
+                for j in range(PAIR):
+                    times_zi(s - 1, j, rz[j], p_rows[s - 1])
             if s < ROUNDS:
                 zj_q[s] = quantise("zj", zj_grouped)
-            if 0 <= s - 1 < ROUNDS:
-                times_zi(s - 1, 1, rz[1], p_rows[s - 1])
             if 0 <= s - 2 < ROUNDS:
                 p_q[s - 2] = quantise("p", p_grouped)
             for g in d_pairs:

@@ -25,7 +25,7 @@ D_PAIRS = R_TILES // PAIR
 WORDS = HIDDEN // 2
 HALVES = WORDS // P
 LOAD_GROUPS = ((0, 1), (1, 2), (2, 3), (3, 4), (4, 8))
-FINE_ROUNDS = 3
+FINE_ROUNDS = 4
 D_STEPS = ((0, 1), (2,), (3,))
 WARM_UP = 4
 WARM_STEPS = 2

@@ -180,7 +180,7 @@ def tile_dedicomdecoder_kernel(tc, z_i, z_j, R_words, R_scales, D, out):
             p_flip = psum_p.tile([P, HALVES, PAIR * P], F32)
             flip_words(p_flip, p_rows[:], 1)
             p_grouped = work.tile([P, PAIR * P * PACK], BF16, align_bytes=64)
-            regroup(nc.scalar.copy if i == 0 else nc.vector.tensor_copy, p_grouped[:], p_flip)
+            regroup(nc.scalar.copy if i <= 1 else nc.vector.tensor_copy, p_grouped[:], p_flip)
             return p_grouped
 
         def second_product(i, p_q):

from contextlib import ExitStack

import concourse.mybir as mybir
from concourse.masks import make_identity

BF16 = mybir.dt.bfloat16
F32 = mybir.dt.float32
I32 = mybir.dt.int32
U32 = mybir.dt.uint32
U8 = mybir.dt.uint8
FP8X4 = mybir.dt.float8_e4m3fn_x4
MULT = mybir.AluOpType.mult
SIGMOID = mybir.ActivationFunctionType.Sigmoid
SQUARE = mybir.ActivationFunctionType.Square

P = 128
PACK = 4
BATCH, HIDDEN, RELATIONS = 2048, 512, 1024
BANK = 512
B_TILES = BATCH // P
R_TILES = RELATIONS // P
PAIR = 2
ROUNDS = B_TILES // PAIR
D_PAIRS = R_TILES // PAIR
WORDS = HIDDEN // 2
HALVES = WORDS // P
LOAD_GROUPS = ((0, 1), (1, 2), (2, 3), (3, 4), (4, 8))
FINE_ROUNDS = 4
D_STEPS = ((0, 1), (2,), (3,))
WARM_UP = 4
WARM_STEPS = 2

FLOPS = 2 * BATCH * HIDDEN * HIDDEN + 2 * BATCH * HIDDEN * RELATIONS


def tile_dedicomdecoder_kernel(tc, z_i, z_j, R_words, R_scales, D, out):
    nc = tc.nc
    with ExitStack() as ctx:
        consts = ctx.enter_context(tc.tile_pool(name="consts", bufs=1))
        inputs = ctx.enter_context(tc.tile_pool(name="inputs", bufs=1))
        work = ctx.enter_context(tc.tile_pool(name="work", bufs=ROUNDS))
        results = ctx.enter_context(tc.tile_pool(name="results", bufs=B_TILES))
        psum_zj = ctx.enter_context(tc.psum_pool(name="psum_zj", bufs=1))
        psum_p = ctx.enter_context(tc.psum_pool(name="psum_p", bufs=1))
        psum_rz = ctx.enter_context(tc.psum_pool(name="psum_rz", bufs=2))
        psum_scores = ctx.enter_context(tc.psum_pool(name="psum_scores", bufs=4))
        ctx.enter_context(tc.manual_schedule())

        zj_rows = z_j.rearrange("(p n) k -> p n k", n=B_TILES)
        zi_rows = z_i.rearrange("(p n) h -> p n h", n=B_TILES)
        out_rows = out.rearrange("(p n) r -> p n r", n=B_TILES)
        d_rows = D.rearrange("(n p) h -> p n h", p=P)

        zeros = consts.tile([P, BANK], BF16)
        nc.vector.memset(zeros[:], 0.0)
        unread = psum_p.tile([P, BANK], F32, tag="p_flip")

        def matmuls_on_zeros(count):
            for k in range(count):
                nc.tensor.matmul(out=unread[:], lhsT=zeros[:, :P], rhs=zeros[:], start=True, stop=True)

        matmuls_on_zeros(WARM_UP)

        warm_in = consts.tile([P, 1], F32)
        warm_out = consts.tile([P, 1], F32)
        nc.vector.memset(warm_in[:], 0.0)
        nc.scalar.activation(out=warm_out[:], in_=warm_in[:], func=SIGMOID)

        ident = consts.tile([P, P], F32)
        make_identity(nc, ident[:])

        w_words = consts.tile([P, HIDDEN], U32, align_bytes=64)
        w_scales = consts.tile([P, HIDDEN], U8, align_bytes=64)
        d_in = [inputs.tile([P, PAIR, HIDDEN], BF16, name="d_in%d" % g) for g in range(D_PAIRS)]
        zj_in = {a: inputs.tile([P, (b - a) * PAIR, HIDDEN], BF16, name="zj_in%d" % a) for a, b in LOAD_GROUPS}
        zi_in = {a: inputs.tile([P, (b - a) * PAIR, HIDDEN], BF16, name="zi_in%d" % a) for a, b in LOAD_GROUPS}

        def load_rounds(tiles, rows, a):
            if a in tiles:
                count = tiles[a][:].shape[1]
                nc.sync.dma_start(out=tiles[a][:], in_=rows[:, a * PAIR : a * PAIR + count, :])

        def pair_of(tiles, i):
            a = max(first for first in tiles if first <= i)
            return tiles[a][:, (i - a) * PAIR : (i - a + 1) * PAIR, :]

        def load_w():
            for r in range(4):
                nc.sync.dma_start(
                    out=w_scales[:].bitcast(I32)[r:P:32, :], in_=R_scales[0].bitcast(I32)[r:16:4, :]
                )
            nc.sync.dma_start(
                out=w_words[:].bitcast(I32), in_=R_words[0].rearrange("p n t -> p (n t)").bitcast(I32)
            )

        nc.vector.memset(w_scales[:].bitcast(I32), 0)
        for s in range(ROUNDS + 1):
            load_rounds(zj_in, zj_rows, s)
            if s == 1:
                load_w()
            if s < len(D_STEPS):
                for g in D_STEPS[s]:
                    nc.sync.dma_start(out=d_in[g][:], in_=d_rows[:, g * PAIR : (g + 1) * PAIR, :])
            load_rounds(zi_in, zi_rows, s - 1)

        def flip_words(flipped, rows, step):
            for j in range(PAIR):
                words = rows[:, j, :].bitcast(F32)
                for u in range(HALVES):
                    picked = words[:, u:WORDS:2] if step == 2 else words[:, u * P : (u + 1) * P]
                    nc.tensor.transpose(flipped[:, u, j * P : (j + 1) * P], picked, ident[:])

        def regroup(engine_copy, grouped, flipped):
            engine_copy(
                out=grouped.bitcast(F32).rearrange("p (n u) -> p n u", u=HALVES),
                in_=flipped[:].rearrange("p u n -> p n u"),
            )

        d2_grouped = consts.tile([P, D_PAIRS, PAIR * P * PACK], BF16, align_bytes=64)
        d2_words = consts.tile([P, RELATIONS], U32, align_bytes=64)
        d2_scales = consts.tile([P, RELATIONS], U8, align_bytes=64)

        def square_rows(g):
            d2_rows = inputs.tile([P, PAIR, HIDDEN], BF16, name="d2_rows%d" % g)
            nc.vector.tensor_tensor(out=d2_rows[:], in0=d_in[g][:], in1=d_in[g][:], op=MULT)
            return d2_rows

        def flip_d(g, s, d2_rows):
            d_flip = psum_scores.tile([P, HALVES, PAIR * P], F32, tag="scores")
            flip_words(d_flip, d_in[g][:] if d2_rows is None else d2_rows[:], 1)
            if s < WARM_STEPS:
                matmuls_on_zeros(1)
            if d2_rows is None:
                nc.scalar.activation(
                    out=d2_grouped[:, g].rearrange("p (n u e) -> p n u e", u=HALVES, e=2),
                    in_=d_flip[:].rearrange("p u n -> p (u n)").bitcast(BF16).rearrange("p (u n e) -> p n u e", u=HALVES, e=2),
                    func=SQUARE,
                )
            else:
                regroup(nc.scalar.copy, d2_grouped[:, g], d_flip)

        def quantise_d2(g):
            cols = slice(g * PAIR * P, (g + 1) * PAIR * P)
            nc.vector.quantize_mx(out=d2_words[:, cols].bitcast(FP8X4), scales=d2_scales[:, cols], in_=d2_grouped[:, g])

        def flip_zj(i):
            zj_flip = psum_zj.tile([P, HALVES, PAIR * P], F32)
            flip_words(zj_flip, pair_of(zj_in, i), 2)
            if i < WARM_STEPS:
                matmuls_on_zeros(1)
            zj_grouped = work.tile([P, PAIR * P * PACK], BF16, align_bytes=64)
            regroup(nc.scalar.copy, zj_grouped[:], zj_flip)
            return zj_grouped

        def quantise(label, grouped):
            words = work.tile([P, PAIR * P], U32, name=label + "_words", align_bytes=64)
            scales = work.tile([P, PAIR * P], U8, name=label + "_scales", align_bytes=64)
            nc.vector.quantize_mx(out=words[:].bitcast(FP8X4), scales=scales[:], in_=grouped[:])
            return words, scales

        def first_product(j, zj_q):
            zj_words, zj_scales = zj_q
            b_cols = slice(j * P, (j + 1) * P)
            rz = psum_rz.tile([P, HIDDEN], F32)
            nc.tensor.matmul_mx(
                out=rz[:],
                lhsT=zj_words[:, b_cols].bitcast(FP8X4),
                lhsT_scale=zj_scales[:, b_cols],
                rhs=w_words[:].bitcast(FP8X4),
                rhs_scale=w_scales[:],
                start=True,
                stop=True,
            )
            return rz

        def times_zi(i, j, rz, p_rows):
            nc.vector.tensor_tensor(out=p_rows[:, j, :], in0=rz[:], in1=pair_of(zi_in, i)[:, j, :], op=MULT)

        def flip_p(i, p_rows):
            p_flip = psum_p.tile([P, HALVES, PAIR * P], F32)
            flip_words(p_flip, p_rows[:], 1)
            p_grouped = work.tile([P, PAIR * P * PACK], BF16, align_bytes=64)
            regroup(nc.scalar.copy if i <= 1 else nc.vector.tensor_copy, p_grouped[:], p_flip)
            return p_grouped

        def second_product(i, p_q):
            p_words, p_scales = p_q
            for j in range(PAIR):
                b_cols = slice(j * P, (j + 1) * P)
                result = results.tile([P, RELATIONS], F32)
                for half in range(RELATIONS // BANK):
                    r_cols = slice(half * BANK, (half + 1) * BANK)
                    scores = psum_scores.tile([P, BANK], F32, tag="scores")
                    nc.tensor.matmul_mx(
                        out=scores[:],
                        lhsT=p_words[:, b_cols].bitcast(FP8X4),
                        lhsT_scale=p_scales[:, b_cols],
                        rhs=d2_words[:, r_cols].bitcast(FP8X4),
                        rhs_scale=d2_scales[:, r_cols],
                        start=True,
                        stop=True,
                    )
                    nc.scalar.activation(out=result[:, r_cols], in_=scores[:], func=SIGMOID)
                    if i >= ROUNDS - FINE_ROUNDS:
                        nc.sync.dma_start(out=out_rows[:, i * PAIR + j, r_cols], in_=result[:, r_cols])
                if i < ROUNDS - FINE_ROUNDS:
                    nc.sync.dma_start(out=out_rows[:, i * PAIR + j, :], in_=result[:])

        zj_q = {}
        p_rows = {}
        p_q = {}
        for s in range(ROUNDS + 3):
            d_pairs = D_STEPS[s] if s < len(D_STEPS) else ()
            d2_rows = {g: square_rows(g) if s == 0 else None for g in d_pairs}
            if s < ROUNDS:
                zj_grouped = flip_zj(s)
            if 0 <= s - 2 < ROUNDS:
                p_grouped = flip_p(s - 2, p_rows[s - 2])
            if 0 <= s - 1 < ROUNDS:
                rz = [first_product(j, zj_q[s - 1]) for j in range(PAIR)]
            for g in d_pairs:
                flip_d(g, s, d2_rows[g])
            if 0 <= s - 1 < ROUNDS:
                p_rows[s - 1] = work.tile([P, PAIR, HIDDEN], BF16, name="p_rows")
                for j in range(PAIR):
                    times_zi(s - 1, j, rz[j], p_rows[s - 1])
            if s < ROUNDS:
                zj_q[s] = quantise("zj", zj_grouped)
            if 0 <= s - 2 < ROUNDS:
                p_q[s - 2] = quantise("p", p_grouped)
            for g in d_pairs:
                quantise_d2(g)
            if s >= 3:
                second_product(s - 3, p_q[s - 3])
